import numpy as np
import ml_dtypes


def mxq(x, axis, fmt="e4m3"):
    dtype, down = {"e4m3": (ml_dtypes.float8_e4m3fn, 7), "e5m2": (ml_dtypes.float8_e5m2, 14)}[fmt]
    v = np.moveaxis(np.asarray(x, np.float32).astype(ml_dtypes.bfloat16).astype(np.float64), axis, -1)
    blocks = v.reshape(v.shape[:-1] + (-1, 32))
    amax = np.abs(blocks).max(-1, keepdims=True)
    byte = np.maximum(np.where(amax > 0, np.frexp(amax)[1] - 1 + 127, 0) - down, 1)
    scale = np.exp2(byte - 127.0)
    codes = (blocks / scale).astype(np.float32).astype(dtype).astype(np.float64)
    return np.moveaxis((codes * scale).reshape(v.shape), -1, axis)


WIDE = False


def mx_kscale(k):
    if not WIDE:
        return np.ones(k)
    levels = np.array([10, -10, 5, -5, 0])
    a = np.random.permutation(np.resize(levels, k // 512 * 4)).reshape(k // 512, 4)
    idx = np.arange(k)
    return np.exp2(a[idx // 512, idx % 128 // 32])


BF16 = ml_dtypes.bfloat16


def bf(x):
    return np.asarray(x, np.float32).astype(BF16)


def f64(x):
    return np.asarray(x).astype(np.float64)


B, L, DIMIN, WIDTH, N_HEADS, N_EMBDS = 8, 1024, 512, 512, 8, 64
LAM = 1.0 / (4 * DIMIN)
XS = 10.0
SD = np.sqrt(DIMIN / WIDTH)
ZP = XS / (SD * np.sqrt(WIDTH * DIMIN))


def setup_inputs():
    s = mx_kscale(DIMIN)
    codes = np.maximum(np.random.standard_normal((B, L, WIDTH)), 0.0) * np.sqrt(2.0)
    coef = np.random.standard_normal((B, L, 1))
    return {"x_res": bf(np.random.standard_normal((B, L, DIMIN)) * XS * s),
            "z_pred": bf(codes * coef * ZP),
            "D": bf(np.random.standard_normal((WIDTH, DIMIN)) * SD / s[None, :]),
            "b": bf(np.random.standard_normal((1, DIMIN)) * 0.5 / s)}


def reference(x_res, z_pred, D, b):
    Df = f64(D)
    z_novel = np.maximum(mxq(f64(x_res) * LAM, 2, "e4m3") @ mxq(Df, 1, "e4m3").T, 0.0)
    return (mxq(z_novel + f64(z_pred), 2, "e4m3") @ mxq(Df, 0, "e4m3")) + f64(b)

@@ -1,0 +1,236 @@
+from contextlib import ExitStack
+
+import concourse.mybir as mybir
+from concourse.masks import make_identity
+
+F32 = mybir.dt.float32
+BF16 = mybir.dt.bfloat16
+U32 = mybir.dt.uint32
+U8 = mybir.dt.uint8
+FP8X4 = mybir.dt.float8_e4m3fn_x4
+ALU = mybir.AluOpType
+ACTF = mybir.ActivationFunctionType
+
+P = 128
+TOKENS = 8192
+DIM = 512
+LAM = 1.0 / 2048.0
+ROUND_TILES = 4
+ROUNDS = TOKENS // (P * ROUND_TILES)
+STEPS = 2 * ROUNDS
+LOAD_BUFS = 8
+MANUAL = True
+USE_POOL = True
+
+FLOPS = 2 * 2 * TOKENS * DIM * DIM
+
+
+def tile_originaltemporalsae_pb_t_kernel(tc, x_res, z_pred, D, b, out):
+    nc = tc.nc
+    x_v = x_res.flatten_outer_dims().rearrange("(r p j) d -> r p (j d)", p=P, j=ROUND_TILES)
+    z_v = z_pred.flatten_outer_dims().rearrange("(r p j) d -> r p (j d)", p=P, j=ROUND_TILES)
+    o_v = out.flatten_outer_dims().rearrange("(r p j) d -> r p (j d)", p=P, j=ROUND_TILES)
+
+    with ExitStack() as ctx:
+        const = ctx.enter_context(tc.tile_pool(name="const", bufs=1))
+        loads = ctx.enter_context(tc.tile_pool(name="loads", bufs=LOAD_BUFS))
+        work = ctx.enter_context(tc.tile_pool(name="work", bufs=4))
+        outs = ctx.enter_context(tc.tile_pool(name="outs", bufs=4))
+        psum = ctx.enter_context(tc.psum_pool(name="psum", bufs=2))
+        if MANUAL:
+            ctx.enter_context(tc.manual_schedule())
+
+        x_sb = {}
+        z_sb = {}
+        tx_ps = {}
+        tz_ps = {}
+        xg_sb = {}
+        zt_sb = {}
+        xq_sb = {}
+        xs_sb = {}
+        s1_ps = {}
+        sg_sb = {}
+        sq_sb = {}
+        ss_sb = {}
+        s2_ps = {}
+        o_sb = {}
+
+        def load(r):
+            if r >= ROUNDS:
+                return
+            x_sb[r] = loads.tile([P, ROUND_TILES, DIM], BF16, name="x_sb", tag="x_sb")
+            nc.sync.dma_start(out=x_sb[r][:].rearrange("p j d -> p (j d)"), in_=x_v[r])
+            z_sb[r] = loads.tile([P, ROUND_TILES, DIM], BF16, name="z_sb", tag="z_sb")
+            nc.sync.dma_start(out=z_sb[r][:].rearrange("p j d -> p (j d)"), in_=z_v[r])
+
+        ident = const.tile([P, P], F32, name="ident")
+        make_identity(nc, ident[:])
+        ones = const.tile([P, P], BF16, name="ones")
+        nc.vector.memset(ones[:], 1.0)
+        b_row = const.tile([P, DIM], BF16, name="b_row")
+        nc.vector.memset(b_row[:], 0.0)
+
+        d_nat = const.tile([P, 4, DIM], BF16, name="d_nat")
+        nc.sync.dma_start(
+            out=d_nat[:].rearrange("m (u e) d -> m u (e d)", u=2),
+            in_=D.rearrange("(u m e) d -> m u (e d)", u=2, e=2),
+        )
+        load(0)
+        nc.sync.dma_start(out=b_row[0:1, :], in_=b)
+        for r in range(1, LOAD_BUFS):
+            load(r)
+
+        d2g = const.tile([P, DIM, 4], BF16, name="d2g", align_bytes=64)
+        nc.vector.tensor_copy(out=d2g[:], in_=d_nat[:].rearrange("m t d -> m d t"))
+        d2q = const.tile([P, DIM], U32, name="d2q", align_bytes=64)
+        d2s = const.tile([P, DIM], U8, name="d2s", align_bytes=64)
+
+        d1g = const.tile([P, 4, P, 4], BF16, name="d1g", align_bytes=64)
+        d1g32 = d1g[:].bitcast(F32)
+        d_nat32 = d_nat[:].bitcast(F32)
+        for hh in range(2):
+            dt_ps = psum.tile([P, 2, 2, P], F32, name="dt_ps", tag=("tx", "tz")[hh])
+            for tt in range(2):
+                for u in range(2):
+                    nc.tensor.transpose(dt_ps[:, tt, u, :], d_nat32[:, 2 * hh + tt, u * P : (u + 1) * P], ident[:])
+            nc.vector.tensor_copy(
+                out=d1g32[:, 2 * hh : 2 * hh + 2, :, :], in_=dt_ps[:].rearrange("p t u m -> p t m u")
+            )
+        d1q = const.tile([P, 4, P], U32, name="d1q", align_bytes=64)
+        d1s = const.tile([P, 4, P], U8, name="d1s", align_bytes=64)
+        nc.vector.quantize_mx(
+            out=d1q[:].rearrange("p t m -> p (t m)").bitcast(FP8X4),
+            scales=d1s[:].rearrange("p t m -> p (t m)"),
+            in_=d1g[:].rearrange("p t m k -> p (t m k)"),
+        )
+        nc.vector.quantize_mx(out=d2q[:].bitcast(FP8X4), scales=d2s[:], in_=d2g[:].rearrange("p d t -> p (d t)"))
+
+        b_bc = const.tile([P, DIM], F32, name="b_bc")
+
+        def transposes(s):
+            if s >= STEPS:
+                return
+            r, h = divmod(s, 2)
+            tx_ps[s] = psum.tile([P, 2, 2, P], F32, name="tx", tag="tx")
+            tz_ps[s] = psum.tile([P, 2, 2, P], F32, name="tz", tag="tz")
+            for src, dst in ((x_sb[r], tx_ps[s]), (z_sb[r], tz_ps[s])):
+                src32 = src[:].bitcast(F32)
+                for jj in range(2):
+                    for u in range(2):
+                        nc.tensor.transpose(dst[:, jj, u, :], src32[:, 2 * h + jj, u * P : (u + 1) * P], ident[:])
+
+        def evacuate(s):
+            if s >= STEPS:
+                return
+            xg_sb[s] = work.tile([P, 2, DIM], BF16, name="xg", tag="xg", align_bytes=64)
+            for jj in range(2):
+                nc.scalar.activation(
+                    out=xg_sb[s][:, jj, :].rearrange("p (c u e) -> p c u e", u=2, e=2),
+                    in_=tx_ps[s][:, jj, :, :].bitcast(BF16).rearrange("p u (c e) -> p c u e", e=2),
+                    func=ACTF.Copy,
+                    scale=LAM,
+                )
+            zt_sb[s] = work.tile([P, 2, DIM], BF16, name="zt", tag="zt", bufs=5)
+            nc.scalar.copy(
+                out=zt_sb[s][:].bitcast(F32).rearrange("p j (c u) -> p j c u", u=2),
+                in_=tz_ps[s][:].rearrange("p j u c -> p j c u"),
+            )
+
+        def quantise_x(s):
+            if s >= STEPS:
+                return
+            xq_sb[s] = work.tile([P, 2 * P], U32, name="xq", tag="xq", align_bytes=64)
+            xs_sb[s] = work.tile([P, 2 * P], U8, name="xs", tag="xs", align_bytes=64)
+            nc.vector.quantize_mx(
+                out=xq_sb[s][:].bitcast(FP8X4), scales=xs_sb[s][:], in_=xg_sb[s][:].rearrange("p j k -> p (j k)")
+            )
+
+        def stage1(s, jj):
+            s1_ps[(s, jj)] = psum.tile([P, 4, P], F32, name="s1", tag="s1")
+            cols = slice(jj * P, (jj + 1) * P)
+            for t in range(4):
+                nc.tensor.matmul_mx(
+                    out=s1_ps[(s, jj)][:, t, :],
+                    lhsT=d1q[:, t, :].bitcast(FP8X4),
+                    lhsT_scale=d1s[:, t, :],
+                    rhs=xq_sb[s][:, cols].bitcast(FP8X4),
+                    rhs_scale=xs_sb[s][:, cols],
+                    start=True,
+                    stop=True,
+                )
+
+        def relu_add(s, jj):
+            if jj == 0:
+                sg_sb[s] = work.tile([P, 2, DIM], BF16, name="sg", tag="sg", align_bytes=64)
+            nc.vector.scalar_tensor_tensor(
+                out=sg_sb[s][:, jj, :].rearrange("p (c t) -> p c t", t=4),
+                in0=s1_ps[(s, jj)][:].rearrange("p t c -> p c t"),
+                scalar=0.0,
+                in1=zt_sb[s][:, jj, :].rearrange("p (c t) -> p c t", t=4),
+                op0=ALU.max,
+                op1=ALU.add,
+            )
+
+        def quantise_s(s):
+            sq_sb[s] = work.tile([P, 2 * P], U32, name="sq", tag="sq", align_bytes=64)
+            ss_sb[s] = work.tile([P, 2 * P], U8, name="ss", tag="ss", align_bytes=64)
+            nc.vector.quantize_mx(
+                out=sq_sb[s][:].bitcast(FP8X4), scales=ss_sb[s][:], in_=sg_sb[s][:].rearrange("p j k -> p (j k)")
+            )
+
+        def stage2(s, jj):
+            s2_ps[(s, jj)] = psum.tile([P, DIM], F32, name="s2", tag="s2")
+            cols = slice(jj * P, (jj + 1) * P)
+            nc.tensor.matmul_mx(
+                out=s2_ps[(s, jj)][:],
+                lhsT=sq_sb[s][:, cols].bitcast(FP8X4),
+                lhsT_scale=ss_sb[s][:, cols],
+                rhs=d2q[:].bitcast(FP8X4),
+                rhs_scale=d2s[:],
+                start=True,
+                stop=True,
+            )
+
+        def finish(s):
+            r, h = divmod(s, 2)
+            if h == 0:
+                o_sb[r] = outs.tile([P, ROUND_TILES, DIM], F32, name="o_sb", tag="o_sb")
+            o0 = o_sb[r][:, 2 * h, :]
+            o1 = o_sb[r][:, 2 * h + 1, :]
+            if USE_POOL:
+                nc.scalar.copy(out=o0, in_=s2_ps[(s, 0)][:])
+            else:
+                nc.vector.tensor_tensor(out=o0, in0=s2_ps[(s, 0)][:], in1=b_bc[:], op=ALU.add)
+            nc.vector.tensor_tensor(out=o1, in0=s2_ps[(s, 1)][:], in1=b_bc[:], op=ALU.add)
+            if USE_POOL:
+                nc.gpsimd.tensor_tensor(out=o0, in0=o0, in1=b_bc[:], op=ALU.add)
+            if h == 1:
+                nc.sync.dma_start(out=o_v[r], in_=o_sb[r][:].rearrange("p j d -> p (j d)"))
+
+        transposes(0)
+        evacuate(0)
+        transposes(1)
+        evacuate(1)
+        quantise_x(0)
+        for i in range(STEPS + 1):
+            if i < STEPS:
+                stage1(i, 0)
+                stage1(i, 1)
+            transposes(i + 2)
+            if i < STEPS:
+                relu_add(i, 0)
+                relu_add(i, 1)
+            quantise_x(i + 1)
+            if i < STEPS:
+                quantise_s(i)
+            if i == 0:
+                b_ps = psum.tile([P, DIM], F32, name="b_ps", tag="s2")
+                nc.tensor.matmul(b_ps[:], lhsT=ones[:], rhs=b_row[:], start=True, stop=True)
+                nc.vector.tensor_copy(out=b_bc[:], in_=b_ps[:])
+            if i >= 1:
+                stage2(i - 1, 0)
+                stage2(i - 1, 1)
+                finish(i - 1)
+            evacuate(i + 2)
+            if i % 2 == 0:
+                load(i // 2 + LOAD_BUFS)

@@ -21,6 +21,8 @@ STEPS = 2 * ROUNDS
 LOAD_BUFS = 8
 MANUAL = True
 USE_POOL = True
+LEAD_T = 3
+LEAD_Q = LEAD_T - 1
 
 FLOPS = 2 * 2 * TOKENS * DIM * DIM
 
@@ -34,7 +36,7 @@ def tile_originaltemporalsae_pb_t_kernel(tc, x_res, z_pred, D, b, out):
     with ExitStack() as ctx:
         const = ctx.enter_context(tc.tile_pool(name="const", bufs=1))
         loads = ctx.enter_context(tc.tile_pool(name="loads", bufs=LOAD_BUFS))
-        work = ctx.enter_context(tc.tile_pool(name="work", bufs=4))
+        work = ctx.enter_context(tc.tile_pool(name="work", bufs=LEAD_T + 2))
         outs = ctx.enter_context(tc.tile_pool(name="outs", bufs=4))
         psum = ctx.enter_context(tc.psum_pool(name="psum", bufs=2))
         if MANUAL:
@@ -55,13 +57,16 @@ def tile_originaltemporalsae_pb_t_kernel(tc, x_res, z_pred, D, b, out):
         s2_ps = {}
         o_sb = {}
 
-        def load(r):
+        def load(r, pieces=1):
             if r >= ROUNDS:
                 return
             x_sb[r] = loads.tile([P, ROUND_TILES, DIM], BF16, name="x_sb", tag="x_sb")
-            nc.sync.dma_start(out=x_sb[r][:].rearrange("p j d -> p (j d)"), in_=x_v[r])
             z_sb[r] = loads.tile([P, ROUND_TILES, DIM], BF16, name="z_sb", tag="z_sb")
-            nc.sync.dma_start(out=z_sb[r][:].rearrange("p j d -> p (j d)"), in_=z_v[r])
+            width = ROUND_TILES * DIM // pieces
+            for k in range(pieces):
+                cols = slice(k * width, (k + 1) * width)
+                nc.sync.dma_start(out=x_sb[r][:].rearrange("p j d -> p (j d)")[:, cols], in_=x_v[r][:, cols])
+                nc.sync.dma_start(out=z_sb[r][:].rearrange("p j d -> p (j d)")[:, cols], in_=z_v[r][:, cols])
 
         ident = const.tile([P, P], F32, name="ident")
         make_identity(nc, ident[:])
@@ -75,7 +80,7 @@ def tile_originaltemporalsae_pb_t_kernel(tc, x_res, z_pred, D, b, out):
             out=d_nat[:].rearrange("m (u e) d -> m u (e d)", u=2),
             in_=D.rearrange("(u m e) d -> m u (e d)", u=2, e=2),
         )
-        load(0)
+        load(0, pieces=2)
         nc.sync.dma_start(out=b_row[0:1, :], in_=b)
         for r in range(1, LOAD_BUFS):
             load(r)
@@ -93,9 +98,7 @@ def tile_originaltemporalsae_pb_t_kernel(tc, x_res, z_pred, D, b, out):
             for tt in range(2):
                 for u in range(2):
                     nc.tensor.transpose(dt_ps[:, tt, u, :], d_nat32[:, 2 * hh + tt, u * P : (u + 1) * P], ident[:])
-            nc.vector.tensor_copy(
-                out=d1g32[:, 2 * hh : 2 * hh + 2, :, :], in_=dt_ps[:].rearrange("p t u m -> p t m u")
-            )
+            nc.scalar.copy(out=d1g32[:, 2 * hh : 2 * hh + 2, :, :], in_=dt_ps[:].rearrange("p t u m -> p t m u"))
         d1q = const.tile([P, 4, P], U32, name="d1q", align_bytes=64)
         d1s = const.tile([P, 4, P], U8, name="d1s", align_bytes=64)
         nc.vector.quantize_mx(
@@ -103,8 +106,6 @@ def tile_originaltemporalsae_pb_t_kernel(tc, x_res, z_pred, D, b, out):
             scales=d1s[:].rearrange("p t m -> p (t m)"),
             in_=d1g[:].rearrange("p t m k -> p (t m k)"),
         )
-        nc.vector.quantize_mx(out=d2q[:].bitcast(FP8X4), scales=d2s[:], in_=d2g[:].rearrange("p d t -> p (d t)"))
-
         b_bc = const.tile([P, DIM], F32, name="b_bc")
 
         def transposes(s):
@@ -119,30 +120,40 @@ def tile_originaltemporalsae_pb_t_kernel(tc, x_res, z_pred, D, b, out):
                     for u in range(2):
                         nc.tensor.transpose(dst[:, jj, u, :], src32[:, 2 * h + jj, u * P : (u + 1) * P], ident[:])
 
-        def evacuate(s):
+        def evacuate_x(s, jj):
             if s >= STEPS:
                 return
-            xg_sb[s] = work.tile([P, 2, DIM], BF16, name="xg", tag="xg", align_bytes=64)
-            for jj in range(2):
-                nc.scalar.activation(
-                    out=xg_sb[s][:, jj, :].rearrange("p (c u e) -> p c u e", u=2, e=2),
-                    in_=tx_ps[s][:, jj, :, :].bitcast(BF16).rearrange("p u (c e) -> p c u e", e=2),
-                    func=ACTF.Copy,
-                    scale=LAM,
-                )
-            zt_sb[s] = work.tile([P, 2, DIM], BF16, name="zt", tag="zt", bufs=5)
-            nc.scalar.copy(
-                out=zt_sb[s][:].bitcast(F32).rearrange("p j (c u) -> p j c u", u=2),
-                in_=tz_ps[s][:].rearrange("p j u c -> p j c u"),
+            if jj == 0:
+                xg_sb[s] = work.tile([P, 2, DIM], BF16, name="xg", tag="xg", align_bytes=64)
+            nc.scalar.activation(
+                out=xg_sb[s][:, jj, :].rearrange("p (c u e) -> p c u e", u=2, e=2),
+                in_=tx_ps[s][:, jj, :, :].bitcast(BF16).rearrange("p u (c e) -> p c u e", e=2),
+                func=ACTF.Copy,
+                scale=LAM,
             )
 
-        def quantise_x(s):
+        def evacuate_z(s, on_vector=False):
             if s >= STEPS:
                 return
-            xq_sb[s] = work.tile([P, 2 * P], U32, name="xq", tag="xq", align_bytes=64)
-            xs_sb[s] = work.tile([P, 2 * P], U8, name="xs", tag="xs", align_bytes=64)
+            zt_sb[s] = work.tile([P, 2, DIM], BF16, name="zt", tag="zt", bufs=LEAD_T + 3)
+            dst = zt_sb[s][:].bitcast(F32).rearrange("p j (c u) -> p j c u", u=2)
+            src = tz_ps[s][:].rearrange("p j u c -> p j c u")
+            if on_vector:
+                nc.vector.tensor_copy(out=dst, in_=src)
+            else:
+                nc.scalar.copy(out=dst, in_=src)
+
+        def quantise_x(s, first=0, count=2):
+            if s >= STEPS:
+                return
+            if first == 0:
+                xq_sb[s] = work.tile([P, 2 * P], U32, name="xq", tag="xq", align_bytes=64)
+                xs_sb[s] = work.tile([P, 2 * P], U8, name="xs", tag="xs", align_bytes=64)
+            cols = slice(first * P, (first + count) * P)
             nc.vector.quantize_mx(
-                out=xq_sb[s][:].bitcast(FP8X4), scales=xs_sb[s][:], in_=xg_sb[s][:].rearrange("p j k -> p (j k)")
+                out=xq_sb[s][:, cols].bitcast(FP8X4),
+                scales=xs_sb[s][:, cols],
+                in_=xg_sb[s][:, first : first + count, :].rearrange("p j k -> p (j k)"),
             )
 
         def stage1(s, jj):
@@ -161,7 +172,7 @@ def tile_originaltemporalsae_pb_t_kernel(tc, x_res, z_pred, D, b, out):
 
         def relu_add(s, jj):
             if jj == 0:
-                sg_sb[s] = work.tile([P, 2, DIM], BF16, name="sg", tag="sg", align_bytes=64)
+                sg_sb[s] = work.tile([P, 2, DIM], BF16, name="sg", tag="sg", align_bytes=64, bufs=3)
             nc.vector.scalar_tensor_tensor(
                 out=sg_sb[s][:, jj, :].rearrange("p (c t) -> p c t", t=4),
                 in0=s1_ps[(s, jj)][:].rearrange("p t c -> p c t"),
@@ -172,8 +183,8 @@ def tile_originaltemporalsae_pb_t_kernel(tc, x_res, z_pred, D, b, out):
             )
 
         def quantise_s(s):
-            sq_sb[s] = work.tile([P, 2 * P], U32, name="sq", tag="sq", align_bytes=64)
-            ss_sb[s] = work.tile([P, 2 * P], U8, name="ss", tag="ss", align_bytes=64)
+            sq_sb[s] = work.tile([P, 2 * P], U32, name="sq", tag="sq", align_bytes=64, bufs=3)
+            ss_sb[s] = work.tile([P, 2 * P], U8, name="ss", tag="ss", align_bytes=64, bufs=3)
             nc.vector.quantize_mx(
                 out=sq_sb[s][:].bitcast(FP8X4), scales=ss_sb[s][:], in_=sg_sb[s][:].rearrange("p j k -> p (j k)")
             )
@@ -191,46 +202,81 @@ def tile_originaltemporalsae_pb_t_kernel(tc, x_res, z_pred, D, b, out):
                 stop=True,
             )
 
-        def finish(s):
+        def store(r, first, count):
+            cols = slice(first * DIM, (first + count) * DIM)
+            nc.sync.dma_start(out=o_v[r][:, cols], in_=o_sb[r][:].rearrange("p j d -> p (j d)")[:, cols])
+
+        def finish_scalar(s):
             r, h = divmod(s, 2)
             if h == 0:
                 o_sb[r] = outs.tile([P, ROUND_TILES, DIM], F32, name="o_sb", tag="o_sb")
+            if USE_POOL and s != STEPS - 1:
+                nc.scalar.copy(out=o_sb[r][:, 2 * h, :], in_=s2_ps[(s, 0)][:])
+
+        def finish_rest(s):
+            r, h = divmod(s, 2)
             o0 = o_sb[r][:, 2 * h, :]
             o1 = o_sb[r][:, 2 * h + 1, :]
-            if USE_POOL:
-                nc.scalar.copy(out=o0, in_=s2_ps[(s, 0)][:])
+            last = s == STEPS - 1
+            if USE_POOL and not last:
+                nc.gpsimd.tensor_tensor(out=o0, in0=o0, in1=b_bc[:], op=ALU.add)
             else:
                 nc.vector.tensor_tensor(out=o0, in0=s2_ps[(s, 0)][:], in1=b_bc[:], op=ALU.add)
+                if last:
+                    store(r, 2, 1)
             nc.vector.tensor_tensor(out=o1, in0=s2_ps[(s, 1)][:], in1=b_bc[:], op=ALU.add)
-            if USE_POOL:
-                nc.gpsimd.tensor_tensor(out=o0, in0=o0, in1=b_bc[:], op=ALU.add)
-            if h == 1:
-                nc.sync.dma_start(out=o_v[r], in_=o_sb[r][:].rearrange("p j d -> p (j d)"))
+            if last:
+                store(r, 3, 1)
+            elif r == ROUNDS - 1:
+                store(r, 0, 2)
+            elif h == 1:
+                store(r, 0, 4)
+
+        def evacuate(s):
+            evacuate_x(s, 0)
+            evacuate_x(s, 1)
+            evacuate_z(s)
 
         transposes(0)
-        evacuate(0)
+        evacuate_x(0, 0)
+        quantise_x(0, 0, 1)
+        evacuate_x(0, 1)
+        quantise_x(0, 1, 1)
+        evacuate_z(0)
         transposes(1)
         evacuate(1)
-        quantise_x(0)
         for i in range(STEPS + 1):
+            ahead = range(2, LEAD_T + 1) if i == 0 else (i + LEAD_T,)
             if i < STEPS:
                 stage1(i, 0)
                 stage1(i, 1)
-            transposes(i + 2)
+            for s in ahead:
+                transposes(s)
             if i < STEPS:
                 relu_add(i, 0)
                 relu_add(i, 1)
-            quantise_x(i + 1)
-            if i < STEPS:
-                quantise_s(i)
             if i == 0:
+                quantise_x(1)
+                quantise_s(0)
+                nc.vector.quantize_mx(
+                    out=d2q[:].bitcast(FP8X4), scales=d2s[:], in_=d2g[:].rearrange("p d t -> p (d t)")
+                )
                 b_ps = psum.tile([P, DIM], F32, name="b_ps", tag="s2")
                 nc.tensor.matmul(b_ps[:], lhsT=ones[:], rhs=b_row[:], start=True, stop=True)
                 nc.vector.tensor_copy(out=b_bc[:], in_=b_ps[:])
             if i >= 1:
                 stage2(i - 1, 0)
                 stage2(i - 1, 1)
-                finish(i - 1)
-            evacuate(i + 2)
+                finish_scalar(i - 1)
+            for s in ahead:
+                evacuate(s)
+            if i == 0:
+                for s in range(2, LEAD_Q + 1):
+                    quantise_x(s)
+            else:
+                quantise_x(i + LEAD_Q)
+                if i < STEPS:
+                    quantise_s(i)
+                finish_rest(i - 1)
             if i % 2 == 0:
                 load(i // 2 + LOAD_BUFS)

@@ -23,6 +23,8 @@ MANUAL = True
 USE_POOL = True
 LEAD_T = 3
 LEAD_Q = LEAD_T - 1
+EXTRA_EVERY = 0
+EXTRA_STEPS = ()
 
 FLOPS = 2 * 2 * TOKENS * DIM * DIM
 
@@ -37,7 +39,7 @@ def tile_originaltemporalsae_pb_t_kernel(tc, x_res, z_pred, D, b, out):
         const = ctx.enter_context(tc.tile_pool(name="const", bufs=1))
         loads = ctx.enter_context(tc.tile_pool(name="loads", bufs=LOAD_BUFS))
         work = ctx.enter_context(tc.tile_pool(name="work", bufs=LEAD_T + 2))
-        outs = ctx.enter_context(tc.tile_pool(name="outs", bufs=4))
+        outs = ctx.enter_context(tc.tile_pool(name="outs", bufs=8))
         psum = ctx.enter_context(tc.psum_pool(name="psum", bufs=2))
         if MANUAL:
             ctx.enter_context(tc.manual_schedule())
@@ -75,13 +77,15 @@ def tile_originaltemporalsae_pb_t_kernel(tc, x_res, z_pred, D, b, out):
         b_row = const.tile([P, DIM], BF16, name="b_row")
         nc.vector.memset(b_row[:], 0.0)
 
+        nc.scalar.dma_start(out=b_row[0:1, :], in_=b)
+        b_bc = const.tile([P, DIM], F32, name="b_bc")
+
         d_nat = const.tile([P, 4, DIM], BF16, name="d_nat")
         nc.sync.dma_start(
             out=d_nat[:].rearrange("m (u e) d -> m u (e d)", u=2),
             in_=D.rearrange("(u m e) d -> m u (e d)", u=2, e=2),
         )
         load(0, pieces=2)
-        nc.sync.dma_start(out=b_row[0:1, :], in_=b)
         for r in range(1, LOAD_BUFS):
             load(r)
 
@@ -89,6 +93,7 @@ def tile_originaltemporalsae_pb_t_kernel(tc, x_res, z_pred, D, b, out):
         nc.vector.tensor_copy(out=d2g[:], in_=d_nat[:].rearrange("m t d -> m d t"))
         d2q = const.tile([P, DIM], U32, name="d2q", align_bytes=64)
         d2s = const.tile([P, DIM], U8, name="d2s", align_bytes=64)
+        nc.vector.quantize_mx(out=d2q[:].bitcast(FP8X4), scales=d2s[:], in_=d2g[:].rearrange("p d t -> p (d t)"))
 
         d1g = const.tile([P, 4, P, 4], BF16, name="d1g", align_bytes=64)
         d1g32 = d1g[:].bitcast(F32)
@@ -106,7 +111,6 @@ def tile_originaltemporalsae_pb_t_kernel(tc, x_res, z_pred, D, b, out):
             scales=d1s[:].rearrange("p t m -> p (t m)"),
             in_=d1g[:].rearrange("p t m k -> p (t m k)"),
         )
-        b_bc = const.tile([P, DIM], F32, name="b_bc")
 
         def transposes(s):
             if s >= STEPS:
@@ -118,16 +122,18 @@ def tile_originaltemporalsae_pb_t_kernel(tc, x_res, z_pred, D, b, out):
                 src32 = src[:].bitcast(F32)
                 for jj in range(2):
                     for u in range(2):
-                        nc.tensor.transpose(dst[:, jj, u, :], src32[:, 2 * h + jj, u * P : (u + 1) * P], ident[:])
+                        nc.tensor.transpose(dst[:, u, jj, :], src32[:, 2 * h + jj, u * P : (u + 1) * P], ident[:])
 
-        def evacuate_x(s, jj):
+        def evacuate_x(s, first=0, count=2):
             if s >= STEPS:
                 return
-            if jj == 0:
+            if first == 0:
                 xg_sb[s] = work.tile([P, 2, DIM], BF16, name="xg", tag="xg", align_bytes=64)
             nc.scalar.activation(
-                out=xg_sb[s][:, jj, :].rearrange("p (c u e) -> p c u e", u=2, e=2),
-                in_=tx_ps[s][:, jj, :, :].bitcast(BF16).rearrange("p u (c e) -> p c u e", e=2),
+                out=xg_sb[s][:, first : first + count, :].rearrange("p j (c u e) -> p (j c) u e", u=2, e=2),
+                in_=tx_ps[s][:, :, first : first + count, :]
+                .bitcast(BF16)
+                .rearrange("p u j (c e) -> p (j c) u e", e=2),
                 func=ACTF.Copy,
                 scale=LAM,
             )
@@ -136,8 +142,8 @@ def tile_originaltemporalsae_pb_t_kernel(tc, x_res, z_pred, D, b, out):
             if s >= STEPS:
                 return
             zt_sb[s] = work.tile([P, 2, DIM], BF16, name="zt", tag="zt", bufs=LEAD_T + 3)
-            dst = zt_sb[s][:].bitcast(F32).rearrange("p j (c u) -> p j c u", u=2)
-            src = tz_ps[s][:].rearrange("p j u c -> p j c u")
+            dst = zt_sb[s][:].bitcast(F32).rearrange("p j (c u) -> p (j c) u", u=2)
+            src = tz_ps[s][:].rearrange("p u j c -> p (j c) u")
             if on_vector:
                 nc.vector.tensor_copy(out=dst, in_=src)
             else:
@@ -206,44 +212,51 @@ def tile_originaltemporalsae_pb_t_kernel(tc, x_res, z_pred, D, b, out):
             cols = slice(first * DIM, (first + count) * DIM)
             nc.sync.dma_start(out=o_v[r][:, cols], in_=o_sb[r][:].rearrange("p j d -> p (j d)")[:, cols])
 
+        def via_scalar(s, jj):
+            if not USE_POOL or s == STEPS - 1:
+                return False
+            return jj == 0 or s in EXTRA_STEPS or (EXTRA_EVERY > 0 and s % EXTRA_EVERY == EXTRA_EVERY - 1)
+
         def finish_scalar(s):
             r, h = divmod(s, 2)
             if h == 0:
                 o_sb[r] = outs.tile([P, ROUND_TILES, DIM], F32, name="o_sb", tag="o_sb")
-            if USE_POOL and s != STEPS - 1:
-                nc.scalar.copy(out=o_sb[r][:, 2 * h, :], in_=s2_ps[(s, 0)][:])
+            for jj in range(2):
+                if via_scalar(s, jj):
+                    nc.scalar.copy(out=o_sb[r][:, 2 * h + jj, :], in_=s2_ps[(s, jj)][:])
 
         def finish_rest(s):
             r, h = divmod(s, 2)
-            o0 = o_sb[r][:, 2 * h, :]
-            o1 = o_sb[r][:, 2 * h + 1, :]
             last = s == STEPS - 1
-            if USE_POOL and not last:
-                nc.gpsimd.tensor_tensor(out=o0, in0=o0, in1=b_bc[:], op=ALU.add)
-            else:
-                nc.vector.tensor_tensor(out=o0, in0=s2_ps[(s, 0)][:], in1=b_bc[:], op=ALU.add)
+            for jj in range(2):
+                o_t = o_sb[r][:, 2 * h + jj, :]
+                if via_scalar(s, jj):
+                    nc.gpsimd.tensor_tensor(out=o_t, in0=o_t, in1=b_bc[:], op=ALU.add)
+                else:
+                    nc.vector.tensor_tensor(out=o_t, in0=s2_ps[(s, jj)][:], in1=b_bc[:], op=ALU.add)
                 if last:
-                    store(r, 2, 1)
-            nc.vector.tensor_tensor(out=o1, in0=s2_ps[(s, 1)][:], in1=b_bc[:], op=ALU.add)
+                    store(r, 2 + jj, 1)
             if last:
-                store(r, 3, 1)
-            elif r == ROUNDS - 1:
+                return
+            if r == ROUNDS - 1:
                 store(r, 0, 2)
             elif h == 1:
                 store(r, 0, 4)
 
         def evacuate(s):
-            evacuate_x(s, 0)
-            evacuate_x(s, 1)
+            evacuate_x(s)
             evacuate_z(s)
 
         transposes(0)
-        evacuate_x(0, 0)
+        evacuate_x(0, 0, 1)
         quantise_x(0, 0, 1)
-        evacuate_x(0, 1)
+        evacuate_x(0, 1, 1)
         quantise_x(0, 1, 1)
         evacuate_z(0)
         transposes(1)
+        b_ps = psum.tile([P, DIM], F32, name="b_ps", tag="s2")
+        nc.tensor.matmul(b_ps[:], lhsT=ones[:], rhs=b_row[:], start=True, stop=True)
+        nc.vector.tensor_copy(out=b_bc[:], in_=b_ps[:])
         evacuate(1)
         for i in range(STEPS + 1):
             ahead = range(2, LEAD_T + 1) if i == 0 else (i + LEAD_T,)
@@ -258,12 +271,6 @@ def tile_originaltemporalsae_pb_t_kernel(tc, x_res, z_pred, D, b, out):
             if i == 0:
                 quantise_x(1)
                 quantise_s(0)
-                nc.vector.quantize_mx(
-                    out=d2q[:].bitcast(FP8X4), scales=d2s[:], in_=d2g[:].rearrange("p d t -> p (d t)")
-                )
-                b_ps = psum.tile([P, DIM], F32, name="b_ps", tag="s2")
-                nc.tensor.matmul(b_ps[:], lhsT=ones[:], rhs=b_row[:], start=True, stop=True)
-                nc.vector.tensor_copy(out=b_bc[:], in_=b_ps[:])
             if i >= 1:
                 stage2(i - 1, 0)
                 stage2(i - 1, 1)

@@ -70,21 +70,19 @@ def tile_originaltemporalsae_pb_t_kernel(tc, x_res, z_pred, D, b, out):
                 nc.sync.dma_start(out=x_sb[r][:].rearrange("p j d -> p (j d)")[:, cols], in_=x_v[r][:, cols])
                 nc.sync.dma_start(out=z_sb[r][:].rearrange("p j d -> p (j d)")[:, cols], in_=z_v[r][:, cols])
 
+        b_row = const.tile([P, DIM], BF16, name="b_row")
+        nc.gpsimd.memset(b_row[:], 0.0)
+        nc.scalar.dma_start(out=b_row[0:1, :], in_=b)
         ident = const.tile([P, P], F32, name="ident")
         make_identity(nc, ident[:])
         ones = const.tile([P, P], BF16, name="ones")
         nc.vector.memset(ones[:], 1.0)
-        b_row = const.tile([P, DIM], BF16, name="b_row")
-        nc.vector.memset(b_row[:], 0.0)
-
-        nc.scalar.dma_start(out=b_row[0:1, :], in_=b)
         b_bc = const.tile([P, DIM], F32, name="b_bc")
 
         d_nat = const.tile([P, 4, DIM], BF16, name="d_nat")
-        nc.sync.dma_start(
-            out=d_nat[:].rearrange("m (u e) d -> m u (e d)", u=2),
-            in_=D.rearrange("(u m e) d -> m u (e d)", u=2, e=2),
-        )
+        d_v = D.rearrange("(u m e) d -> u m (e d)", u=2, e=2)
+        for u in range(2):
+            nc.sync.dma_start(out=d_nat[:, 2 * u : 2 * u + 2, :].rearrange("m e d -> m (e d)"), in_=d_v[u])
         load(0, pieces=2)
         for r in range(1, LOAD_BUFS):
             load(r)
@@ -93,7 +91,6 @@ def tile_originaltemporalsae_pb_t_kernel(tc, x_res, z_pred, D, b, out):
         nc.vector.tensor_copy(out=d2g[:], in_=d_nat[:].rearrange("m t d -> m d t"))
         d2q = const.tile([P, DIM], U32, name="d2q", align_bytes=64)
         d2s = const.tile([P, DIM], U8, name="d2s", align_bytes=64)
-        nc.vector.quantize_mx(out=d2q[:].bitcast(FP8X4), scales=d2s[:], in_=d2g[:].rearrange("p d t -> p (d t)"))
 
         d1g = const.tile([P, 4, P, 4], BF16, name="d1g", align_bytes=64)
         d1g32 = d1g[:].bitcast(F32)
@@ -250,6 +247,7 @@ def tile_originaltemporalsae_pb_t_kernel(tc, x_res, z_pred, D, b, out):
         transposes(0)
         evacuate_x(0, 0, 1)
         quantise_x(0, 0, 1)
+        nc.vector.quantize_mx(out=d2q[:].bitcast(FP8X4), scales=d2s[:], in_=d2g[:].rearrange("p d t -> p (d t)"))
         evacuate_x(0, 1, 1)
         quantise_x(0, 1, 1)
         evacuate_z(0)

@@ -24,6 +24,7 @@ USE_POOL = True
 LEAD_T = 3
 LEAD_Q = LEAD_T - 1
 EXTRA_EVERY = 0
+NO_POOL_TAIL = 3
 EXTRA_STEPS = ()
 
 FLOPS = 2 * 2 * TOKENS * DIM * DIM
@@ -210,7 +211,7 @@ def tile_originaltemporalsae_pb_t_kernel(tc, x_res, z_pred, D, b, out):
             nc.sync.dma_start(out=o_v[r][:, cols], in_=o_sb[r][:].rearrange("p j d -> p (j d)")[:, cols])
 
         def via_scalar(s, jj):
-            if not USE_POOL or s == STEPS - 1:
+            if not USE_POOL or s >= STEPS - NO_POOL_TAIL:
                 return False
             return jj == 0 or s in EXTRA_STEPS or (EXTRA_EVERY > 0 and s % EXTRA_EVERY == EXTRA_EVERY - 1)
 

from contextlib import ExitStack

import concourse.mybir as mybir
from concourse.masks import make_identity

F32 = mybir.dt.float32
BF16 = mybir.dt.bfloat16
U32 = mybir.dt.uint32
U8 = mybir.dt.uint8
FP8X4 = mybir.dt.float8_e4m3fn_x4
ALU = mybir.AluOpType
ACTF = mybir.ActivationFunctionType

P = 128
TOKENS = 8192
DIM = 512
LAM = 1.0 / 2048.0
ROUND_TILES = 4
ROUNDS = TOKENS // (P * ROUND_TILES)
STEPS = 2 * ROUNDS
LOAD_BUFS = 8
MANUAL = True
USE_POOL = True
LEAD_T = 3
LEAD_Q = LEAD_T - 1
EXTRA_EVERY = 0
NO_POOL_TAIL = 3
EXTRA_STEPS = ()

FLOPS = 2 * 2 * TOKENS * DIM * DIM


def tile_originaltemporalsae_pb_t_kernel(tc, x_res, z_pred, D, b, out):
    nc = tc.nc
    x_v = x_res.flatten_outer_dims().rearrange("(r p j) d -> r p (j d)", p=P, j=ROUND_TILES)
    z_v = z_pred.flatten_outer_dims().rearrange("(r p j) d -> r p (j d)", p=P, j=ROUND_TILES)
    o_v = out.flatten_outer_dims().rearrange("(r p j) d -> r p (j d)", p=P, j=ROUND_TILES)

    with ExitStack() as ctx:
        const = ctx.enter_context(tc.tile_pool(name="const", bufs=1))
        loads = ctx.enter_context(tc.tile_pool(name="loads", bufs=LOAD_BUFS))
        work = ctx.enter_context(tc.tile_pool(name="work", bufs=LEAD_T + 2))
        outs = ctx.enter_context(tc.tile_pool(name="outs", bufs=8))
        psum = ctx.enter_context(tc.psum_pool(name="psum", bufs=2))
        if MANUAL:
            ctx.enter_context(tc.manual_schedule())

        x_sb = {}
        z_sb = {}
        tx_ps = {}
        tz_ps = {}
        xg_sb = {}
        zt_sb = {}
        xq_sb = {}
        xs_sb = {}
        s1_ps = {}
        sg_sb = {}
        sq_sb = {}
        ss_sb = {}
        s2_ps = {}
        o_sb = {}

        def load(r, pieces=1):
            if r >= ROUNDS:
                return
            x_sb[r] = loads.tile([P, ROUND_TILES, DIM], BF16, name="x_sb", tag="x_sb")
            z_sb[r] = loads.tile([P, ROUND_TILES, DIM], BF16, name="z_sb", tag="z_sb")
            width = ROUND_TILES * DIM // pieces
            for k in range(pieces):
                cols = slice(k * width, (k + 1) * width)
                nc.sync.dma_start(out=x_sb[r][:].rearrange("p j d -> p (j d)")[:, cols], in_=x_v[r][:, cols])
                nc.sync.dma_start(out=z_sb[r][:].rearrange("p j d -> p (j d)")[:, cols], in_=z_v[r][:, cols])

        b_row = const.tile([P, DIM], BF16, name="b_row")
        nc.gpsimd.memset(b_row[:], 0.0)
        nc.scalar.dma_start(out=b_row[0:1, :], in_=b)
        ident = const.tile([P, P], F32, name="ident")
        make_identity(nc, ident[:])
        ones = const.tile([P, P], BF16, name="ones")
        nc.vector.memset(ones[:], 1.0)
        b_bc = const.tile([P, DIM], F32, name="b_bc")

        d_nat = const.tile([P, 4, DIM], BF16, name="d_nat")
        d_v = D.rearrange("(u m e) d -> u m (e d)", u=2, e=2)
        for u in range(2):
            nc.sync.dma_start(out=d_nat[:, 2 * u : 2 * u + 2, :].rearrange("m e d -> m (e d)"), in_=d_v[u])
        load(0, pieces=2)
        for r in range(1, LOAD_BUFS):
            load(r)

        d2g = const.tile([P, DIM, 4], BF16, name="d2g", align_bytes=64)
        nc.vector.tensor_copy(out=d2g[:], in_=d_nat[:].rearrange("m t d -> m d t"))
        d2q = const.tile([P, DIM], U32, name="d2q", align_bytes=64)
        d2s = const.tile([P, DIM], U8, name="d2s", align_bytes=64)

        d1g = const.tile([P, 4, P, 4], BF16, name="d1g", align_bytes=64)
        d1g32 = d1g[:].bitcast(F32)
        d_nat32 = d_nat[:].bitcast(F32)
        for hh in range(2):
            dt_ps = psum.tile([P, 2, 2, P], F32, name="dt_ps", tag=("tx", "tz")[hh])
            for tt in range(2):
                for u in range(2):
                    nc.tensor.transpose(dt_ps[:, tt, u, :], d_nat32[:, 2 * hh + tt, u * P : (u + 1) * P], ident[:])
            nc.scalar.copy(out=d1g32[:, 2 * hh : 2 * hh + 2, :, :], in_=dt_ps[:].rearrange("p t u m -> p t m u"))
        d1q = const.tile([P, 4, P], U32, name="d1q", align_bytes=64)
        d1s = const.tile([P, 4, P], U8, name="d1s", align_bytes=64)
        nc.vector.quantize_mx(
            out=d1q[:].rearrange("p t m -> p (t m)").bitcast(FP8X4),
            scales=d1s[:].rearrange("p t m -> p (t m)"),
            in_=d1g[:].rearrange("p t m k -> p (t m k)"),
        )

        def transposes(s):
            if s >= STEPS:
                return
            r, h = divmod(s, 2)
            tx_ps[s] = psum.tile([P, 2, 2, P], F32, name="tx", tag="tx")
            tz_ps[s] = psum.tile([P, 2, 2, P], F32, name="tz", tag="tz")
            for src, dst in ((x_sb[r], tx_ps[s]), (z_sb[r], tz_ps[s])):
                src32 = src[:].bitcast(F32)
                for jj in range(2):
                    for u in range(2):
                        nc.tensor.transpose(dst[:, u, jj, :], src32[:, 2 * h + jj, u * P : (u + 1) * P], ident[:])

        def evacuate_x(s, first=0, count=2):
            if s >= STEPS:
                return
            if first == 0:
                xg_sb[s] = work.tile([P, 2, DIM], BF16, name="xg", tag="xg", align_bytes=64)
            nc.scalar.activation(
                out=xg_sb[s][:, first : first + count, :].rearrange("p j (c u e) -> p (j c) u e", u=2, e=2),
                in_=tx_ps[s][:, :, first : first + count, :]
                .bitcast(BF16)
                .rearrange("p u j (c e) -> p (j c) u e", e=2),
                func=ACTF.Copy,
                scale=LAM,
            )

        def evacuate_z(s, on_vector=False):
            if s >= STEPS:
                return
            zt_sb[s] = work.tile([P, 2, DIM], BF16, name="zt", tag="zt", bufs=LEAD_T + 3)
            dst = zt_sb[s][:].bitcast(F32).rearrange("p j (c u) -> p (j c) u", u=2)
            src = tz_ps[s][:].rearrange("p u j c -> p (j c) u")
            if on_vector:
                nc.vector.tensor_copy(out=dst, in_=src)
            else:
                nc.scalar.copy(out=dst, in_=src)

        def quantise_x(s, first=0, count=2):
            if s >= STEPS:
                return
            if first == 0:
                xq_sb[s] = work.tile([P, 2 * P], U32, name="xq", tag="xq", align_bytes=64)
                xs_sb[s] = work.tile([P, 2 * P], U8, name="xs", tag="xs", align_bytes=64)
            cols = slice(first * P, (first + count) * P)
            nc.vector.quantize_mx(
                out=xq_sb[s][:, cols].bitcast(FP8X4),
                scales=xs_sb[s][:, cols],
                in_=xg_sb[s][:, first : first + count, :].rearrange("p j k -> p (j k)"),
            )

        def stage1(s, jj):
            s1_ps[(s, jj)] = psum.tile([P, 4, P], F32, name="s1", tag="s1")
            cols = slice(jj * P, (jj + 1) * P)
            for t in range(4):
                nc.tensor.matmul_mx(
                    out=s1_ps[(s, jj)][:, t, :],
                    lhsT=d1q[:, t, :].bitcast(FP8X4),
                    lhsT_scale=d1s[:, t, :],
                    rhs=xq_sb[s][:, cols].bitcast(FP8X4),
                    rhs_scale=xs_sb[s][:, cols],
                    start=True,
                    stop=True,
                )

        def relu_add(s, jj):
            if jj == 0:
                sg_sb[s] = work.tile([P, 2, DIM], BF16, name="sg", tag="sg", align_bytes=64, bufs=3)
            nc.vector.scalar_tensor_tensor(
                out=sg_sb[s][:, jj, :].rearrange("p (c t) -> p c t", t=4),
                in0=s1_ps[(s, jj)][:].rearrange("p t c -> p c t"),
                scalar=0.0,
                in1=zt_sb[s][:, jj, :].rearrange("p (c t) -> p c t", t=4),
                op0=ALU.max,
                op1=ALU.add,
            )

        def quantise_s(s):
            sq_sb[s] = work.tile([P, 2 * P], U32, name="sq", tag="sq", align_bytes=64, bufs=3)
            ss_sb[s] = work.tile([P, 2 * P], U8, name="ss", tag="ss", align_bytes=64, bufs=3)
            nc.vector.quantize_mx(
                out=sq_sb[s][:].bitcast(FP8X4), scales=ss_sb[s][:], in_=sg_sb[s][:].rearrange("p j k -> p (j k)")
            )

        def stage2(s, jj):
            s2_ps[(s, jj)] = psum.tile([P, DIM], F32, name="s2", tag="s2")
            cols = slice(jj * P, (jj + 1) * P)
            nc.tensor.matmul_mx(
                out=s2_ps[(s, jj)][:],
                lhsT=sq_sb[s][:, cols].bitcast(FP8X4),
                lhsT_scale=ss_sb[s][:, cols],
                rhs=d2q[:].bitcast(FP8X4),
                rhs_scale=d2s[:],
                start=True,
                stop=True,
            )

        def store(r, first, count):
            cols = slice(first * DIM, (first + count) * DIM)
            nc.sync.dma_start(out=o_v[r][:, cols], in_=o_sb[r][:].rearrange("p j d -> p (j d)")[:, cols])

        def via_scalar(s, jj):
            if not USE_POOL or s >= STEPS - NO_POOL_TAIL:
                return False
            return jj == 0 or s in EXTRA_STEPS or (EXTRA_EVERY > 0 and s % EXTRA_EVERY == EXTRA_EVERY - 1)

        def finish_scalar(s):
            r, h = divmod(s, 2)
            if h == 0:
                o_sb[r] = outs.tile([P, ROUND_TILES, DIM], F32, name="o_sb", tag="o_sb")
            for jj in range(2):
                if via_scalar(s, jj):
                    nc.scalar.copy(out=o_sb[r][:, 2 * h + jj, :], in_=s2_ps[(s, jj)][:])

        def finish_rest(s):
            r, h = divmod(s, 2)
            last = s == STEPS - 1
            for jj in range(2):
                o_t = o_sb[r][:, 2 * h + jj, :]
                if via_scalar(s, jj):
                    nc.gpsimd.tensor_tensor(out=o_t, in0=o_t, in1=b_bc[:], op=ALU.add)
                else:
                    nc.vector.tensor_tensor(out=o_t, in0=s2_ps[(s, jj)][:], in1=b_bc[:], op=ALU.add)
                if last:
                    store(r, 2 + jj, 1)
            if last:
                return
            if r == ROUNDS - 1:
                store(r, 0, 2)
            elif h == 1:
                store(r, 0, 4)

        def evacuate(s):
            evacuate_x(s)
            evacuate_z(s)

        transposes(0)
        evacuate_x(0, 0, 1)
        quantise_x(0, 0, 1)
        nc.vector.quantize_mx(out=d2q[:].bitcast(FP8X4), scales=d2s[:], in_=d2g[:].rearrange("p d t -> p (d t)"))
        evacuate_x(0, 1, 1)
        quantise_x(0, 1, 1)
        evacuate_z(0)
        transposes(1)
        b_ps = psum.tile([P, DIM], F32, name="b_ps", tag="s2")
        nc.tensor.matmul(b_ps[:], lhsT=ones[:], rhs=b_row[:], start=True, stop=True)
        nc.vector.tensor_copy(out=b_bc[:], in_=b_ps[:])
        evacuate(1)
        for i in range(STEPS + 1):
            ahead = range(2, LEAD_T + 1) if i == 0 else (i + LEAD_T,)
            if i < STEPS:
                stage1(i, 0)
                stage1(i, 1)
            for s in ahead:
                transposes(s)
            if i < STEPS:
                relu_add(i, 0)
                relu_add(i, 1)
            if i == 0:
                quantise_x(1)
                quantise_s(0)
            if i >= 1:
                stage2(i - 1, 0)
                stage2(i - 1, 1)
                finish_scalar(i - 1)
            for s in ahead:
                evacuate(s)
            if i == 0:
                for s in range(2, LEAD_Q + 1):
                    quantise_x(s)
            else:
                quantise_x(i + LEAD_Q)
                if i < STEPS:
                    quantise_s(i)
                finish_rest(i - 1)
            if i % 2 == 0:
                load(i // 2 + LOAD_BUFS)
